import numpy as np
import ml_dtypes


def mxq(x, axis, fmt="e4m3"):
    dtype, down = {"e4m3": (ml_dtypes.float8_e4m3fn, 7), "e5m2": (ml_dtypes.float8_e5m2, 14)}[fmt]
    v = np.moveaxis(np.asarray(x, np.float32).astype(ml_dtypes.bfloat16).astype(np.float64), axis, -1)
    blocks = v.reshape(v.shape[:-1] + (-1, 32))
    amax = np.abs(blocks).max(-1, keepdims=True)
    byte = np.maximum(np.where(amax > 0, np.frexp(amax)[1] - 1 + 127, 0) - down, 1)
    scale = np.exp2(byte - 127.0)
    codes = (blocks / scale).astype(np.float32).astype(dtype).astype(np.float64)
    return np.moveaxis((codes * scale).reshape(v.shape), -1, axis)


WIDE = False


def mx_kscale(k):
    if not WIDE:
        return np.ones(k)
    levels = np.array([20, -20, 10, -10, 0])
    a = np.random.permutation(np.resize(levels, k // 512 * 4)).reshape(k // 512, 4)
    idx = np.arange(k)
    return np.exp2(a[idx // 512, idx % 128 // 32])


BF16 = ml_dtypes.bfloat16


def bf(x):
    return np.asarray(x, np.float32).astype(BF16)


def f64(x):
    return np.asarray(x).astype(np.float64)


B, N, C, H, F = 2, 256, 512, 4, 2752
D = C // H


def setup_inputs():
    u = mx_kscale(C)
    z = np.random.standard_normal((B, H, D, D)) * np.sqrt((N + N * N / C) / D)
    e = np.exp(z - z.max(-1, keepdims=True))
    attn = e / e.sum(-1, keepdims=True)
    v = np.random.standard_normal((B, H, N, D))
    w_proj = np.random.standard_normal((C, C)) / np.sqrt(C) / u[:, None]
    b_proj = 0.1 * np.random.standard_normal(C)
    shortcut = np.random.standard_normal((B, N, C))
    g = np.random.standard_normal((B, N, C)) * np.exp2(np.random.randint(-12, 1, (B, N, 1))) * 16.0 * u
    return {"attn": bf(attn), "v": bf(v), "w_proj": bf(w_proj), "b_proj": bf(b_proj),
            "shortcut": bf(shortcut), "grad_out": bf(g)}


def reference(attn, v, w_proj, b_proj, shortcut, grad_out):
    dy = mxq(f64(grad_out), 2, "e5m2") @ mxq(f64(w_proj), 0, "e4m3")
    do = dy.reshape(B, H, N, D)
    return do @ f64(attn)

@@ -1,0 +1,139 @@
+import concourse.mybir as mybir
+from concourse.masks import make_identity
+
+F32 = mybir.dt.float32
+BF16 = mybir.dt.bfloat16
+U32 = mybir.dt.uint32
+U8 = mybir.dt.uint8
+E4M3_X4 = mybir.dt.float8_e4m3fn_x4
+E5M2_X4 = mybir.dt.float8_e5m2_x4
+MULT = mybir.AluOpType.mult
+ADD = mybir.AluOpType.add
+
+P = 128
+PACK = 4
+C = 512
+D = 128
+HEADS = 8
+ROWS = 512
+ROW_TILES = ROWS // P
+ROWS_PER_HEAD = ROWS // HEADS
+HEAD_TOKENS = 256
+
+FLOPS = 2 * ROWS * C * C + 2 * HEADS * HEAD_TOKENS * D * D
+BYTES = 2 * (ROWS * C + C * C + HEADS * D * D) + 4 * HEADS * HEAD_TOKENS * D
+
+
+def tile_transposedattentiontransformer_pb_s_kernel(
+    tc, attn, v, w_proj, b_proj, shortcut, grad_out, out
+):
+    nc = tc.nc
+    with (
+        tc.tile_pool(name="keep", bufs=1) as keep,
+        tc.tile_pool(name="g_in", bufs=ROW_TILES) as g_in,
+        tc.tile_pool(name="results", bufs=4) as results,
+        tc.psum_pool(name="psum_g", bufs=2) as psum_g,
+        tc.psum_pool(name="psum_dy", bufs=4) as psum_dy,
+        tc.psum_pool(name="psum_out", bufs=2) as psum_out,
+    ):
+        identity = keep.tile([P, P], F32)
+        make_identity(nc, identity[:])
+
+        w_raw = keep.tile([P, PACK, C], BF16)
+        nc.sync.dma_start(
+            out=w_raw[:].rearrange("p (u e) c -> p u (e c)", u=2),
+            in_=w_proj.rearrange("(u p e) c -> p u (e c)", u=2, e=2),
+        )
+        g_flat = grad_out.flatten_outer_dims()
+        g_rows = []
+        for rt in range(ROW_TILES):
+            g_tile = g_in.tile([P, C], BF16, name="g_tile")
+            nc.sync.dma_start(out=g_tile[:], in_=g_flat[rt * P : (rt + 1) * P, :])
+            g_rows.append(g_tile)
+        attn_bf = keep.tile([P, HEADS, D], BF16)
+        nc.sync.dma_start(out=attn_bf[:], in_=attn.rearrange("b g d e -> d (b g) e"))
+
+        w_grouped = keep.tile([P, C, PACK], BF16, align_bytes=64)
+        nc.vector.tensor_copy(
+            out=w_grouped[:].rearrange("p (c i) t -> p c t i", i=4),
+            in_=w_raw[:].rearrange("p t (c i) -> p c t i", i=4),
+        )
+        w_codes = keep.tile([P, C], U32, align_bytes=64)
+        w_scales = keep.tile([P, C], U8, align_bytes=64)
+        nc.vector.quantize_mx(
+            out=w_codes[:].bitcast(E4M3_X4),
+            scales=w_scales[:],
+            in_=w_grouped[:].rearrange("p c t -> p (c t)"),
+        )
+
+        g_grouped = keep.tile([P, ROWS * PACK], BF16, align_bytes=64)
+        g_grouped_words = g_grouped[:].bitcast(F32).rearrange("p (r u) -> p r u", u=2)
+        g_codes = keep.tile([P, ROWS], U32, align_bytes=64)
+        g_scales = keep.tile([P, ROWS], U8, align_bytes=64)
+        for rt in range(ROW_TILES):
+            rows = slice(rt * P, (rt + 1) * P)
+            g_words = g_rows[rt][:].bitcast(F32)
+            g_t = psum_g.tile([P, 2, P], F32)
+            for u in range(2):
+                nc.tensor.transpose(g_t[:, u, :], g_words[:, u * P : (u + 1) * P], identity[:])
+            nc.scalar.copy(out=g_grouped_words[:, rows, :], in_=g_t[:].rearrange("p u r -> p r u"))
+            nc.vector.quantize_mx(
+                out=g_codes[:, rows].bitcast(E5M2_X4),
+                scales=g_scales[:, rows],
+                in_=g_grouped[:, rt * P * PACK : (rt + 1) * P * PACK],
+            )
+
+        attn_f32 = keep.tile([P, HEADS, D], F32)
+        for half in range(2):
+            heads = slice(half * HEADS // 2, (half + 1) * HEADS // 2)
+            nc.gpsimd.tensor_scalar(
+                out=attn_f32[:, heads, :], in0=attn_bf[:, heads, :],
+                scalar1=1.0, scalar2=0.0, op0=MULT, op1=ADD,
+            )
+
+        do_t = keep.tile([P, HEADS, 2, P], F32)
+        dy_banks = {}
+        for q_lo in range(2):
+            for q_hi in range(2):
+                q = 2 * q_hi + q_lo
+                dy_t = psum_dy.tile([P, ROWS], F32)
+                nc.tensor.matmul_mx(
+                    out=dy_t[:],
+                    lhsT=w_codes[:, q * D : (q + 1) * D].bitcast(E4M3_X4),
+                    lhsT_scale=w_scales[:, q * D : (q + 1) * D],
+                    rhs=g_codes[:].bitcast(E5M2_X4),
+                    rhs_scale=g_scales[:],
+                    start=True,
+                    stop=True,
+                )
+                dy_banks[(q_lo, q_hi)] = dy_t
+        for half in range(2):
+            heads = slice(half * HEADS // 2, (half + 1) * HEADS // 2)
+            cols = slice(half * ROWS // 2, (half + 1) * ROWS // 2)
+            for q_lo in range(2):
+                for q_hi in range(2):
+                    copy = nc.vector.tensor_copy if q_hi == 0 else nc.scalar.copy
+                    copy(
+                        out=do_t[:, heads, q_lo, q_hi * ROWS_PER_HEAD : (q_hi + 1) * ROWS_PER_HEAD],
+                        in_=dy_banks[(q_lo, q_hi)][:, cols].rearrange(
+                            "p (g r) -> p g r", r=ROWS_PER_HEAD
+                        ),
+                    )
+
+        out_view = out.rearrange("b g (r a l) e -> (b g) a r (l e)", a=2, l=2)
+        for head in range(HEADS):
+            product = psum_out.tile([P, 2, D], F32)
+            for q_lo in range(2):
+                nc.tensor.matmul(
+                    out=product[:, q_lo, :],
+                    lhsT=do_t[:, head, q_lo, :],
+                    rhs=attn_f32[:, head, :],
+                    start=True,
+                    stop=True,
+                )
+            result = results.tile([P, 2 * D], F32)
+            copy = nc.vector.tensor_copy if head % 2 == 0 else nc.scalar.copy
+            copy(out=result[:], in_=product[:].rearrange("p l e -> p (l e)"))
+            for q_hi in range(2):
+                part = slice(q_hi * ROWS_PER_HEAD, (q_hi + 1) * ROWS_PER_HEAD)
+                nc.sync.dma_start(out=out_view[head, q_hi], in_=result[part, :])

@@ -31,10 +31,9 @@ def tile_transposedattentiontransformer_pb_s_kernel(
     with (
         tc.tile_pool(name="keep", bufs=1) as keep,
         tc.tile_pool(name="g_in", bufs=ROW_TILES) as g_in,
-        tc.tile_pool(name="results", bufs=4) as results,
-        tc.psum_pool(name="psum_g", bufs=2) as psum_g,
+        tc.tile_pool(name="results", bufs=HEADS) as results,
         tc.psum_pool(name="psum_dy", bufs=4) as psum_dy,
-        tc.psum_pool(name="psum_out", bufs=2) as psum_out,
+        tc.psum_pool(name="psum_small", bufs=4) as psum_small,
     ):
         identity = keep.tile([P, P], F32)
         make_identity(nc, identity[:])
@@ -73,7 +72,7 @@ def tile_transposedattentiontransformer_pb_s_kernel(
         for rt in range(ROW_TILES):
             rows = slice(rt * P, (rt + 1) * P)
             g_words = g_rows[rt][:].bitcast(F32)
-            g_t = psum_g.tile([P, 2, P], F32)
+            g_t = psum_small.tile([P, 2, P], F32, tag="small")
             for u in range(2):
                 nc.tensor.transpose(g_t[:, u, :], g_words[:, u * P : (u + 1) * P], identity[:])
             nc.scalar.copy(out=g_grouped_words[:, rows, :], in_=g_t[:].rearrange("p u r -> p r u"))
@@ -122,7 +121,7 @@ def tile_transposedattentiontransformer_pb_s_kernel(
 
         out_view = out.rearrange("b g (r a l) e -> (b g) a r (l e)", a=2, l=2)
         for head in range(HEADS):
-            product = psum_out.tile([P, 2, D], F32)
+            product = psum_small.tile([P, 2, D], F32, tag="small")
             for q_lo in range(2):
                 nc.tensor.matmul(
                     out=product[:, q_lo, :],

@@ -31,39 +31,35 @@ def tile_transposedattentiontransformer_pb_s_kernel(
     with (
         tc.tile_pool(name="keep", bufs=1) as keep,
         tc.tile_pool(name="g_in", bufs=ROW_TILES) as g_in,
+        tc.tile_pool(name="w_in", bufs=C // D) as w_in,
+        tc.tile_pool(name="do_pool", bufs=4) as do_pool,
         tc.tile_pool(name="results", bufs=HEADS) as results,
         tc.psum_pool(name="psum_dy", bufs=4) as psum_dy,
         tc.psum_pool(name="psum_small", bufs=4) as psum_small,
+        tc.manual_schedule(),
     ):
         identity = keep.tile([P, P], F32)
         make_identity(nc, identity[:])
 
-        w_raw = keep.tile([P, PACK, C], BF16)
-        nc.sync.dma_start(
-            out=w_raw[:].rearrange("p (u e) c -> p u (e c)", u=2),
-            in_=w_proj.rearrange("(u p e) c -> p u (e c)", u=2, e=2),
-        )
         g_flat = grad_out.flatten_outer_dims()
         g_rows = []
         for rt in range(ROW_TILES):
             g_tile = g_in.tile([P, C], BF16, name="g_tile")
             nc.sync.dma_start(out=g_tile[:], in_=g_flat[rt * P : (rt + 1) * P, :])
             g_rows.append(g_tile)
+        w_view = w_proj.rearrange("(p t) c -> p t c", t=PACK)
+        w_raw = {}
+        for q_lo in range(2):
+            for q_hi in range(2):
+                chunk = slice((2 * q_hi + q_lo) * D, (2 * q_hi + q_lo + 1) * D)
+                w_chunk = w_in.tile([P, PACK, D], BF16, name="w_chunk")
+                nc.sync.dma_start(out=w_chunk[:], in_=w_view[:, :, chunk])
+                w_raw[(q_lo, q_hi)] = w_chunk
         attn_bf = keep.tile([P, HEADS, D], BF16)
-        nc.sync.dma_start(out=attn_bf[:], in_=attn.rearrange("b g d e -> d (b g) e"))
-
-        w_grouped = keep.tile([P, C, PACK], BF16, align_bytes=64)
-        nc.vector.tensor_copy(
-            out=w_grouped[:].rearrange("p (c i) t -> p c t i", i=4),
-            in_=w_raw[:].rearrange("p t (c i) -> p c t i", i=4),
-        )
-        w_codes = keep.tile([P, C], U32, align_bytes=64)
-        w_scales = keep.tile([P, C], U8, align_bytes=64)
-        nc.vector.quantize_mx(
-            out=w_codes[:].bitcast(E4M3_X4),
-            scales=w_scales[:],
-            in_=w_grouped[:].rearrange("p c t -> p (c t)"),
-        )
+        attn_view = attn.rearrange("b g d e -> d (b g) e")
+        for half in range(2):
+            heads = slice(half * HEADS // 2, (half + 1) * HEADS // 2)
+            nc.sync.dma_start(out=attn_bf[:, heads, :], in_=attn_view[:, heads, :])
 
         g_grouped = keep.tile([P, ROWS * PACK], BF16, align_bytes=64)
         g_grouped_words = g_grouped[:].bitcast(F32).rearrange("p (r u) -> p r u", u=2)
@@ -71,49 +67,81 @@ def tile_transposedattentiontransformer_pb_s_kernel(
         g_scales = keep.tile([P, ROWS], U8, align_bytes=64)
         for rt in range(ROW_TILES):
             rows = slice(rt * P, (rt + 1) * P)
-            g_words = g_rows[rt][:].bitcast(F32)
+            g_words = g_rows[rt][:].bitcast(F32).rearrange("r (p u) -> r u p", u=2)
             g_t = psum_small.tile([P, 2, P], F32, tag="small")
             for u in range(2):
-                nc.tensor.transpose(g_t[:, u, :], g_words[:, u * P : (u + 1) * P], identity[:])
+                nc.tensor.transpose(g_t[:, u, :], g_words[:, u, :], identity[:])
             nc.scalar.copy(out=g_grouped_words[:, rows, :], in_=g_t[:].rearrange("p u r -> p r u"))
+
+        def quantise_g(rt):
+            rows = slice(rt * P, (rt + 1) * P)
             nc.vector.quantize_mx(
                 out=g_codes[:, rows].bitcast(E5M2_X4),
                 scales=g_scales[:, rows],
                 in_=g_grouped[:, rt * P * PACK : (rt + 1) * P * PACK],
             )
 
-        attn_f32 = keep.tile([P, HEADS, D], F32)
-        for half in range(2):
-            heads = slice(half * HEADS // 2, (half + 1) * HEADS // 2)
-            nc.gpsimd.tensor_scalar(
-                out=attn_f32[:, heads, :], in0=attn_bf[:, heads, :],
-                scalar1=1.0, scalar2=0.0, op0=MULT, op1=ADD,
+        w_grouped = keep.tile([P, C, PACK], BF16, align_bytes=64)
+        w_codes = keep.tile([P, C], U32, align_bytes=64)
+        w_scales = keep.tile([P, C], U8, align_bytes=64)
+        pass_order = [(q_lo, q_hi) for q_lo in range(2) for q_hi in range(2)]
+
+        def regroup_w(q_lo, q_hi):
+            chunk = slice((2 * q_hi + q_lo) * D, (2 * q_hi + q_lo + 1) * D)
+            nc.vector.tensor_copy(
+                out=w_grouped[:, chunk, :].rearrange("p (c i) t -> p c t i", i=4),
+                in_=w_raw[(q_lo, q_hi)][:].rearrange("p t (c i) -> p c t i", i=4),
             )
 
-        do_t = keep.tile([P, HEADS, 2, P], F32)
+        def quantise_w(q_lo, q_hi):
+            chunk = slice((2 * q_hi + q_lo) * D, (2 * q_hi + q_lo + 1) * D)
+            nc.vector.quantize_mx(
+                out=w_codes[:, chunk].bitcast(E4M3_X4),
+                scales=w_scales[:, chunk],
+                in_=w_grouped[:, chunk, :].rearrange("p c t -> p (c t)"),
+            )
+
+        for rt in range(ROW_TILES - 1):
+            quantise_g(rt)
+        regroup_w(*pass_order[0])
+        quantise_g(ROW_TILES - 1)
+        for i in range(len(pass_order)):
+            if i + 1 < len(pass_order):
+                regroup_w(*pass_order[i + 1])
+            quantise_w(*pass_order[i])
+
         dy_banks = {}
         for q_lo in range(2):
             for q_hi in range(2):
-                q = 2 * q_hi + q_lo
+                chunk = slice((2 * q_hi + q_lo) * D, (2 * q_hi + q_lo + 1) * D)
                 dy_t = psum_dy.tile([P, ROWS], F32)
                 nc.tensor.matmul_mx(
                     out=dy_t[:],
-                    lhsT=w_codes[:, q * D : (q + 1) * D].bitcast(E4M3_X4),
-                    lhsT_scale=w_scales[:, q * D : (q + 1) * D],
+                    lhsT=w_codes[:, chunk].bitcast(E4M3_X4),
+                    lhsT_scale=w_scales[:, chunk],
                     rhs=g_codes[:].bitcast(E5M2_X4),
                     rhs_scale=g_scales[:],
                     start=True,
                     stop=True,
                 )
                 dy_banks[(q_lo, q_hi)] = dy_t
+
+        do_t = {}
+        attn_f32 = keep.tile([P, HEADS, D], F32)
         for half in range(2):
             heads = slice(half * HEADS // 2, (half + 1) * HEADS // 2)
             cols = slice(half * ROWS // 2, (half + 1) * ROWS // 2)
+            nc.gpsimd.tensor_scalar(
+                out=attn_f32[:, heads, :], in0=attn_bf[:, heads, :],
+                scalar1=1.0, scalar2=0.0, op0=MULT, op1=ADD,
+            )
             for q_lo in range(2):
+                do_tile = do_pool.tile([P, HEADS // 2, P], F32, name="do_tile")
+                do_t[(half, q_lo)] = do_tile
                 for q_hi in range(2):
                     copy = nc.vector.tensor_copy if q_hi == 0 else nc.scalar.copy
                     copy(
-                        out=do_t[:, heads, q_lo, q_hi * ROWS_PER_HEAD : (q_hi + 1) * ROWS_PER_HEAD],
+                        out=do_tile[:, :, q_hi * ROWS_PER_HEAD : (q_hi + 1) * ROWS_PER_HEAD],
                         in_=dy_banks[(q_lo, q_hi)][:, cols].rearrange(
                             "p (g r) -> p g r", r=ROWS_PER_HEAD
                         ),
@@ -125,7 +153,7 @@ def tile_transposedattentiontransformer_pb_s_kernel(
             for q_lo in range(2):
                 nc.tensor.matmul(
                     out=product[:, q_lo, :],
-                    lhsT=do_t[:, head, q_lo, :],
+                    lhsT=do_t[(head // (HEADS // 2), q_lo)][:, head % (HEADS // 2), :],
                     rhs=attn_f32[:, head, :],
                     start=True,
                     stop=True,

@@ -31,7 +31,6 @@ def tile_transposedattentiontransformer_pb_s_kernel(
     with (
         tc.tile_pool(name="keep", bufs=1) as keep,
         tc.tile_pool(name="g_in", bufs=ROW_TILES) as g_in,
-        tc.tile_pool(name="w_in", bufs=C // D) as w_in,
         tc.tile_pool(name="do_pool", bufs=4) as do_pool,
         tc.tile_pool(name="results", bufs=HEADS) as results,
         tc.psum_pool(name="psum_dy", bufs=4) as psum_dy,
@@ -47,14 +46,8 @@ def tile_transposedattentiontransformer_pb_s_kernel(
             g_tile = g_in.tile([P, C], BF16, name="g_tile")
             nc.sync.dma_start(out=g_tile[:], in_=g_flat[rt * P : (rt + 1) * P, :])
             g_rows.append(g_tile)
-        w_view = w_proj.rearrange("(p t) c -> p t c", t=PACK)
-        w_raw = {}
-        for q_lo in range(2):
-            for q_hi in range(2):
-                chunk = slice((2 * q_hi + q_lo) * D, (2 * q_hi + q_lo + 1) * D)
-                w_chunk = w_in.tile([P, PACK, D], BF16, name="w_chunk")
-                nc.sync.dma_start(out=w_chunk[:], in_=w_view[:, :, chunk])
-                w_raw[(q_lo, q_hi)] = w_chunk
+        w_raw = keep.tile([P, PACK, C], BF16)
+        nc.sync.dma_start(out=w_raw[:], in_=w_proj.rearrange("(p t) c -> p t c", t=PACK))
         attn_bf = keep.tile([P, HEADS, D], BF16)
         attn_view = attn.rearrange("b g d e -> d (b g) e")
         for half in range(2):
@@ -90,7 +83,7 @@ def tile_transposedattentiontransformer_pb_s_kernel(
             chunk = slice((2 * q_hi + q_lo) * D, (2 * q_hi + q_lo + 1) * D)
             nc.vector.tensor_copy(
                 out=w_grouped[:, chunk, :].rearrange("p (c i) t -> p c t i", i=4),
-                in_=w_raw[(q_lo, q_hi)][:].rearrange("p t (c i) -> p c t i", i=4),
+                in_=w_raw[:, :, chunk].rearrange("p t (c i) -> p c t i", i=4),
             )
 
         def quantise_w(q_lo, q_hi):

@@ -24,6 +24,11 @@ FLOPS = 2 * ROWS * C * C + 2 * HEADS * HEAD_TOKENS * D * D
 BYTES = 2 * (ROWS * C + C * C + HEADS * D * D) + 4 * HEADS * HEAD_TOKENS * D
 
 
+HALF_HEADS = HEADS // 2
+HEAD_IDLE_PASSES = 2
+GAP_IDLE_PASSES = 3
+
+
 def tile_transposedattentiontransformer_pb_s_kernel(
     tc, attn, v, w_proj, b_proj, shortcut, grad_out, out
 ):
@@ -37,8 +42,42 @@ def tile_transposedattentiontransformer_pb_s_kernel(
         tc.psum_pool(name="psum_small", bufs=4) as psum_small,
         tc.manual_schedule(),
     ):
+        idle_in = keep.tile([P, D * PACK], BF16, align_bytes=64)
+        nc.gpsimd.memset(idle_in[:], 1.0)
         identity = keep.tile([P, P], F32)
         make_identity(nc, identity[:])
+        idle_g_codes = keep.tile([P, ROWS], U32, align_bytes=64)
+        idle_g_scales = keep.tile([P, ROWS], U8, align_bytes=64)
+        idle_w_codes = keep.tile([P, D], U32, align_bytes=64)
+        idle_w_scales = keep.tile([P, D], U8, align_bytes=64)
+        nc.vector.quantize_mx(
+            out=idle_w_codes[:].bitcast(E4M3_X4), scales=idle_w_scales[:], in_=idle_in[:]
+        )
+        for rt in range(ROW_TILES):
+            nc.vector.quantize_mx(
+                out=idle_g_codes[:, rt * P : (rt + 1) * P].bitcast(E5M2_X4),
+                scales=idle_g_scales[:, rt * P : (rt + 1) * P],
+                in_=idle_in[:],
+            )
+        idle_out = psum_dy.tile([P, ROWS], F32, tag="dy")
+
+        def idle_passes(count):
+            for i in range(count):
+                nc.tensor.matmul_mx(
+                    out=idle_out[:],
+                    lhsT=idle_w_codes[:].bitcast(E4M3_X4),
+                    lhsT_scale=idle_w_scales[:],
+                    rhs=idle_g_codes[:].bitcast(E5M2_X4),
+                    rhs_scale=idle_g_scales[:],
+                    start=True,
+                    stop=True,
+                )
+
+        def columns(q_lo, q_hi):
+            return slice((2 * q_hi + q_lo) * D, (2 * q_hi + q_lo + 1) * D)
+
+        def heads_of(half):
+            return slice(half * HALF_HEADS, (half + 1) * HALF_HEADS)
 
         g_flat = grad_out.flatten_outer_dims()
         g_rows = []
@@ -49,16 +88,17 @@ def tile_transposedattentiontransformer_pb_s_kernel(
         w_raw = keep.tile([P, PACK, C], BF16)
         nc.sync.dma_start(out=w_raw[:], in_=w_proj.rearrange("(p t) c -> p t c", t=PACK))
         attn_bf = keep.tile([P, HEADS, D], BF16)
+        attn_f32 = keep.tile([P, HEADS, D], F32)
         attn_view = attn.rearrange("b g d e -> d (b g) e")
         for half in range(2):
-            heads = slice(half * HEADS // 2, (half + 1) * HEADS // 2)
-            nc.sync.dma_start(out=attn_bf[:, heads, :], in_=attn_view[:, heads, :])
+            nc.sync.dma_start(out=attn_bf[:, heads_of(half), :], in_=attn_view[:, heads_of(half), :])
 
         g_grouped = keep.tile([P, ROWS * PACK], BF16, align_bytes=64)
         g_grouped_words = g_grouped[:].bitcast(F32).rearrange("p (r u) -> p r u", u=2)
         g_codes = keep.tile([P, ROWS], U32, align_bytes=64)
         g_scales = keep.tile([P, ROWS], U8, align_bytes=64)
-        for rt in range(ROW_TILES):
+
+        def transpose_g(rt):
             rows = slice(rt * P, (rt + 1) * P)
             g_words = g_rows[rt][:].bitcast(F32).rearrange("r (p u) -> r u p", u=2)
             g_t = psum_small.tile([P, 2, P], F32, tag="small")
@@ -66,94 +106,122 @@ def tile_transposedattentiontransformer_pb_s_kernel(
                 nc.tensor.transpose(g_t[:, u, :], g_words[:, u, :], identity[:])
             nc.scalar.copy(out=g_grouped_words[:, rows, :], in_=g_t[:].rearrange("p u r -> p r u"))
 
-        def quantise_g(rt):
-            rows = slice(rt * P, (rt + 1) * P)
+        def quantise_g(first, count):
+            rows = slice(first * P, (first + count) * P)
             nc.vector.quantize_mx(
                 out=g_codes[:, rows].bitcast(E5M2_X4),
                 scales=g_scales[:, rows],
-                in_=g_grouped[:, rt * P * PACK : (rt + 1) * P * PACK],
+                in_=g_grouped[:, first * P * PACK : (first + count) * P * PACK],
             )
 
         w_grouped = keep.tile([P, C, PACK], BF16, align_bytes=64)
         w_codes = keep.tile([P, C], U32, align_bytes=64)
         w_scales = keep.tile([P, C], U8, align_bytes=64)
-        pass_order = [(q_lo, q_hi) for q_lo in range(2) for q_hi in range(2)]
 
-        def regroup_w(q_lo, q_hi):
-            chunk = slice((2 * q_hi + q_lo) * D, (2 * q_hi + q_lo + 1) * D)
-            nc.vector.tensor_copy(
-                out=w_grouped[:, chunk, :].rearrange("p (c i) t -> p c t i", i=4),
-                in_=w_raw[:, :, chunk].rearrange("p t (c i) -> p c t i", i=4),
+        def regroup_w(copy, q_lo, q_hi):
+            copy(
+                out=w_grouped[:, columns(q_lo, q_hi), :].rearrange("p (c i) t -> p c t i", i=4),
+                in_=w_raw[:, :, columns(q_lo, q_hi)].rearrange("p t (c i) -> p c t i", i=4),
             )
 
         def quantise_w(q_lo, q_hi):
-            chunk = slice((2 * q_hi + q_lo) * D, (2 * q_hi + q_lo + 1) * D)
             nc.vector.quantize_mx(
-                out=w_codes[:, chunk].bitcast(E4M3_X4),
-                scales=w_scales[:, chunk],
-                in_=w_grouped[:, chunk, :].rearrange("p c t -> p (c t)"),
+                out=w_codes[:, columns(q_lo, q_hi)].bitcast(E4M3_X4),
+                scales=w_scales[:, columns(q_lo, q_hi)],
+                in_=w_grouped[:, columns(q_lo, q_hi), :].rearrange("p c t -> p (c t)"),
             )
 
-        for rt in range(ROW_TILES - 1):
-            quantise_g(rt)
-        regroup_w(*pass_order[0])
-        quantise_g(ROW_TILES - 1)
-        for i in range(len(pass_order)):
-            if i + 1 < len(pass_order):
-                regroup_w(*pass_order[i + 1])
-            quantise_w(*pass_order[i])
-
-        dy_banks = {}
-        for q_lo in range(2):
-            for q_hi in range(2):
-                chunk = slice((2 * q_hi + q_lo) * D, (2 * q_hi + q_lo + 1) * D)
-                dy_t = psum_dy.tile([P, ROWS], F32)
-                nc.tensor.matmul_mx(
-                    out=dy_t[:],
-                    lhsT=w_codes[:, chunk].bitcast(E4M3_X4),
-                    lhsT_scale=w_scales[:, chunk],
-                    rhs=g_codes[:].bitcast(E5M2_X4),
-                    rhs_scale=g_scales[:],
-                    start=True,
-                    stop=True,
-                )
-                dy_banks[(q_lo, q_hi)] = dy_t
-
-        do_t = {}
-        attn_f32 = keep.tile([P, HEADS, D], F32)
-        for half in range(2):
-            heads = slice(half * HEADS // 2, (half + 1) * HEADS // 2)
-            cols = slice(half * ROWS // 2, (half + 1) * ROWS // 2)
+        def widen_attn(half):
             nc.gpsimd.tensor_scalar(
-                out=attn_f32[:, heads, :], in0=attn_bf[:, heads, :],
+                out=attn_f32[:, heads_of(half), :], in0=attn_bf[:, heads_of(half), :],
                 scalar1=1.0, scalar2=0.0, op0=MULT, op1=ADD,
             )
-            for q_lo in range(2):
-                do_tile = do_pool.tile([P, HEADS // 2, P], F32, name="do_tile")
+
+        dy_banks = {}
+
+        def mx_pass(q_lo, q_hi):
+            dy_t = psum_dy.tile([P, ROWS], F32, tag="dy")
+            nc.tensor.matmul_mx(
+                out=dy_t[:],
+                lhsT=w_codes[:, columns(q_lo, q_hi)].bitcast(E4M3_X4),
+                lhsT_scale=w_scales[:, columns(q_lo, q_hi)],
+                rhs=g_codes[:].bitcast(E5M2_X4),
+                rhs_scale=g_scales[:],
+                start=True,
+                stop=True,
+            )
+            dy_banks[(q_lo, q_hi)] = dy_t
+
+        do_t = {}
+
+        def empty_bank(copy, half, q_lo, q_hi):
+            if (half, q_lo) not in do_t:
+                do_tile = do_pool.tile([P, HALF_HEADS, P], F32, name="do_tile")
                 do_t[(half, q_lo)] = do_tile
-                for q_hi in range(2):
-                    copy = nc.vector.tensor_copy if q_hi == 0 else nc.scalar.copy
-                    copy(
-                        out=do_tile[:, :, q_hi * ROWS_PER_HEAD : (q_hi + 1) * ROWS_PER_HEAD],
-                        in_=dy_banks[(q_lo, q_hi)][:, cols].rearrange(
-                            "p (g r) -> p g r", r=ROWS_PER_HEAD
-                        ),
-                    )
+            copy(
+                out=do_t[(half, q_lo)][:, :, q_hi * ROWS_PER_HEAD : (q_hi + 1) * ROWS_PER_HEAD],
+                in_=dy_banks[(q_lo, q_hi)][:, half * ROWS // 2 : (half + 1) * ROWS // 2].rearrange(
+                    "p (g r) -> p g r", r=ROWS_PER_HEAD
+                ),
+            )
 
         out_view = out.rearrange("b g (r a l) e -> (b g) a r (l e)", a=2, l=2)
-        for head in range(HEADS):
-            product = psum_small.tile([P, 2, D], F32, tag="small")
-            for q_lo in range(2):
-                nc.tensor.matmul(
-                    out=product[:, q_lo, :],
-                    lhsT=do_t[(head // (HEADS // 2), q_lo)][:, head % (HEADS // 2), :],
-                    rhs=attn_f32[:, head, :],
-                    start=True,
-                    stop=True,
-                )
+        products = {}
+
+        def product(head, q_lo):
+            if head not in products:
+                product_tile = psum_small.tile([P, 2, D], F32, tag="small")
+                products[head] = product_tile
+            nc.tensor.matmul(
+                out=products[head][:, q_lo, :],
+                lhsT=do_t[(head // HALF_HEADS, q_lo)][:, head % HALF_HEADS, :],
+                rhs=attn_f32[:, head, :],
+                start=True,
+                stop=True,
+            )
+
+        def finish(head):
             result = results.tile([P, 2 * D], F32)
             copy = nc.vector.tensor_copy if head % 2 == 0 else nc.scalar.copy
-            copy(out=result[:], in_=product[:].rearrange("p l e -> p (l e)"))
+            copy(out=result[:], in_=products[head][:].rearrange("p l e -> p (l e)"))
             for q_hi in range(2):
                 part = slice(q_hi * ROWS_PER_HEAD, (q_hi + 1) * ROWS_PER_HEAD)
                 nc.sync.dma_start(out=out_view[head, q_hi], in_=result[part, :])
+
+        on_vector = nc.vector.tensor_copy
+        on_scalar = nc.scalar.copy
+        idle_passes(HEAD_IDLE_PASSES)
+        for rt in range(ROW_TILES):
+            transpose_g(rt)
+        idle_passes(GAP_IDLE_PASSES)
+        for rt in range(ROW_TILES - 1):
+            quantise_g(rt, 1)
+        regroup_w(on_vector, 0, 0)
+        regroup_w(on_scalar, 0, 1)
+        quantise_g(ROW_TILES - 1, 1)
+        quantise_w(0, 0)
+        mx_pass(0, 0)
+        regroup_w(on_vector, 1, 0)
+        regroup_w(on_scalar, 1, 1)
+        quantise_w(0, 1)
+        mx_pass(0, 1)
+        quantise_w(1, 0)
+        mx_pass(1, 0)
+        quantise_w(1, 1)
+        mx_pass(1, 1)
+        widen_attn(0)
+        widen_attn(1)
+        empty_bank(on_scalar, 0, 0, 0)
+        empty_bank(on_scalar, 0, 0, 1)
+        empty_bank(on_vector, 0, 1, 0)
+        empty_bank(on_scalar, 0, 1, 1)
+        empty_bank(on_vector, 1, 0, 0)
+        empty_bank(on_scalar, 1, 0, 1)
+        empty_bank(on_vector, 1, 1, 0)
+        empty_bank(on_scalar, 1, 1, 1)
+        for pair in range(HEADS // 2):
+            for q_lo in range(2):
+                for head in (2 * pair, 2 * pair + 1):
+                    product(head, q_lo)
+                    if q_lo == 1:
+                        finish(head)

@@ -118,10 +118,16 @@ def tile_transposedattentiontransformer_pb_s_kernel(
         w_codes = keep.tile([P, C], U32, align_bytes=64)
         w_scales = keep.tile([P, C], U8, align_bytes=64)
 
-        def regroup_w(copy, q_lo, q_hi):
-            copy(
+        def regroup_w_on_vector(q_lo, q_hi):
+            nc.vector.tensor_copy(
                 out=w_grouped[:, columns(q_lo, q_hi), :].rearrange("p (c i) t -> p c t i", i=4),
                 in_=w_raw[:, :, columns(q_lo, q_hi)].rearrange("p t (c i) -> p c t i", i=4),
+            )
+
+        def regroup_w_on_scalar(q_lo, q_hi):
+            nc.scalar.copy(
+                out=w_grouped[:, columns(q_lo, q_hi), :],
+                in_=w_raw[:, :, columns(q_lo, q_hi)].rearrange("p t c -> p c t"),
             )
 
         def quantise_w(q_lo, q_hi):
@@ -196,13 +202,13 @@ def tile_transposedattentiontransformer_pb_s_kernel(
         idle_passes(GAP_IDLE_PASSES)
         for rt in range(ROW_TILES - 1):
             quantise_g(rt, 1)
-        regroup_w(on_vector, 0, 0)
-        regroup_w(on_scalar, 0, 1)
+        regroup_w_on_vector(0, 0)
+        regroup_w_on_scalar(0, 1)
         quantise_g(ROW_TILES - 1, 1)
         quantise_w(0, 0)
         mx_pass(0, 0)
-        regroup_w(on_vector, 1, 0)
-        regroup_w(on_scalar, 1, 1)
+        regroup_w_on_vector(1, 0)
+        regroup_w_on_scalar(1, 1)
         quantise_w(0, 1)
         mx_pass(0, 1)
         quantise_w(1, 0)

@@ -25,8 +25,7 @@ BYTES = 2 * (ROWS * C + C * C + HEADS * D * D) + 4 * HEADS * HEAD_TOKENS * D
 
 
 HALF_HEADS = HEADS // 2
-HEAD_IDLE_PASSES = 2
-GAP_IDLE_PASSES = 3
+GAP_IDLE_PASSES = 2
 
 
 def tile_transposedattentiontransformer_pb_s_kernel(
@@ -42,22 +41,41 @@ def tile_transposedattentiontransformer_pb_s_kernel(
         tc.psum_pool(name="psum_small", bufs=4) as psum_small,
         tc.manual_schedule(),
     ):
-        idle_in = keep.tile([P, D * PACK], BF16, align_bytes=64)
-        nc.gpsimd.memset(idle_in[:], 1.0)
         identity = keep.tile([P, P], F32)
         make_identity(nc, identity[:])
+
+        def columns(q_lo, q_hi):
+            return slice((2 * q_hi + q_lo) * D, (2 * q_hi + q_lo + 1) * D)
+
+        def heads_of(half):
+            return slice(half * HALF_HEADS, (half + 1) * HALF_HEADS)
+
+        g_flat = grad_out.flatten_outer_dims()
+        g_rows = []
+        for rt in range(ROW_TILES):
+            g_tile = g_in.tile([P, C], BF16, name="g_tile", align_bytes=64)
+            nc.sync.dma_start(out=g_tile[:], in_=g_flat[rt * P : (rt + 1) * P, :])
+            g_rows.append(g_tile)
+        w_raw = keep.tile([P, PACK, C], BF16)
+        nc.sync.dma_start(out=w_raw[:], in_=w_proj.rearrange("(p t) c -> p t c", t=PACK))
+        attn_bf = keep.tile([P, HEADS, D], BF16)
+        attn_f32 = keep.tile([P, HEADS, D], F32)
+        attn_view = attn.rearrange("b g d e -> d (b g) e")
+        for half in range(2):
+            nc.sync.dma_start(out=attn_bf[:, heads_of(half), :], in_=attn_view[:, heads_of(half), :])
+
         idle_g_codes = keep.tile([P, ROWS], U32, align_bytes=64)
         idle_g_scales = keep.tile([P, ROWS], U8, align_bytes=64)
         idle_w_codes = keep.tile([P, D], U32, align_bytes=64)
         idle_w_scales = keep.tile([P, D], U8, align_bytes=64)
         nc.vector.quantize_mx(
-            out=idle_w_codes[:].bitcast(E4M3_X4), scales=idle_w_scales[:], in_=idle_in[:]
+            out=idle_w_codes[:].bitcast(E4M3_X4), scales=idle_w_scales[:], in_=g_rows[0][:]
         )
         for rt in range(ROW_TILES):
             nc.vector.quantize_mx(
                 out=idle_g_codes[:, rt * P : (rt + 1) * P].bitcast(E5M2_X4),
                 scales=idle_g_scales[:, rt * P : (rt + 1) * P],
-                in_=idle_in[:],
+                in_=g_rows[0][:],
             )
         idle_out = psum_dy.tile([P, ROWS], F32, tag="dy")
 
@@ -72,26 +90,6 @@ def tile_transposedattentiontransformer_pb_s_kernel(
                     start=True,
                     stop=True,
                 )
-
-        def columns(q_lo, q_hi):
-            return slice((2 * q_hi + q_lo) * D, (2 * q_hi + q_lo + 1) * D)
-
-        def heads_of(half):
-            return slice(half * HALF_HEADS, (half + 1) * HALF_HEADS)
-
-        g_flat = grad_out.flatten_outer_dims()
-        g_rows = []
-        for rt in range(ROW_TILES):
-            g_tile = g_in.tile([P, C], BF16, name="g_tile")
-            nc.sync.dma_start(out=g_tile[:], in_=g_flat[rt * P : (rt + 1) * P, :])
-            g_rows.append(g_tile)
-        w_raw = keep.tile([P, PACK, C], BF16)
-        nc.sync.dma_start(out=w_raw[:], in_=w_proj.rearrange("(p t) c -> p t c", t=PACK))
-        attn_bf = keep.tile([P, HEADS, D], BF16)
-        attn_f32 = keep.tile([P, HEADS, D], F32)
-        attn_view = attn.rearrange("b g d e -> d (b g) e")
-        for half in range(2):
-            nc.sync.dma_start(out=attn_bf[:, heads_of(half), :], in_=attn_view[:, heads_of(half), :])
 
         g_grouped = keep.tile([P, ROWS * PACK], BF16, align_bytes=64)
         g_grouped_words = g_grouped[:].bitcast(F32).rearrange("p (r u) -> p r u", u=2)
@@ -196,7 +194,6 @@ def tile_transposedattentiontransformer_pb_s_kernel(
 
         on_vector = nc.vector.tensor_copy
         on_scalar = nc.scalar.copy
-        idle_passes(HEAD_IDLE_PASSES)
         for rt in range(ROW_TILES):
             transpose_g(rt)
         idle_passes(GAP_IDLE_PASSES)
@@ -225,9 +222,12 @@ def tile_transposedattentiontransformer_pb_s_kernel(
         empty_bank(on_scalar, 1, 0, 1)
         empty_bank(on_vector, 1, 1, 0)
         empty_bank(on_scalar, 1, 1, 1)
-        for pair in range(HEADS // 2):
+        for q_lo in range(2):
+            for head in range(2):
+                product(head, q_lo)
+                if q_lo == 1:
+                    finish(head)
+        for head in range(2, HEADS):
             for q_lo in range(2):
-                for head in (2 * pair, 2 * pair + 1):
-                    product(head, q_lo)
-                    if q_lo == 1:
-                        finish(head)
+                product(head, q_lo)
+            finish(head)

@@ -7,8 +7,6 @@ U32 = mybir.dt.uint32
 U8 = mybir.dt.uint8
 E4M3_X4 = mybir.dt.float8_e4m3fn_x4
 E5M2_X4 = mybir.dt.float8_e5m2_x4
-MULT = mybir.AluOpType.mult
-ADD = mybir.AluOpType.add
 
 P = 128
 PACK = 4
@@ -135,10 +133,9 @@ def tile_transposedattentiontransformer_pb_s_kernel(
                 in_=w_grouped[:, columns(q_lo, q_hi), :].rearrange("p c t -> p (c t)"),
             )
 
-        def widen_attn(half):
-            nc.gpsimd.tensor_scalar(
-                out=attn_f32[:, heads_of(half), :], in0=attn_bf[:, heads_of(half), :],
-                scalar1=1.0, scalar2=0.0, op0=MULT, op1=ADD,
+        def widen_attn(first, count):
+            nc.vector.tensor_copy(
+                out=attn_f32[:, first : first + count, :], in_=attn_bf[:, first : first + count, :]
             )
 
         dy_banks = {}
@@ -212,16 +209,17 @@ def tile_transposedattentiontransformer_pb_s_kernel(
         mx_pass(1, 0)
         quantise_w(1, 1)
         mx_pass(1, 1)
-        widen_attn(0)
-        widen_attn(1)
+        widen_attn(0, 2)
         empty_bank(on_scalar, 0, 0, 0)
         empty_bank(on_scalar, 0, 0, 1)
         empty_bank(on_vector, 0, 1, 0)
         empty_bank(on_scalar, 0, 1, 1)
+        widen_attn(2, 2)
         empty_bank(on_vector, 1, 0, 0)
         empty_bank(on_scalar, 1, 0, 1)
         empty_bank(on_vector, 1, 1, 0)
         empty_bank(on_scalar, 1, 1, 1)
+        widen_attn(4, 4)
         for q_lo in range(2):
             for head in range(2):
                 product(head, q_lo)

@@ -155,15 +155,28 @@ def tile_transposedattentiontransformer_pb_s_kernel(
 
         do_t = {}
 
-        def empty_bank(copy, half, q_lo, q_hi):
+        def empty_bank(copy, half, q_lo, q_hi, count=HALF_HEADS):
             if (half, q_lo) not in do_t:
                 do_tile = do_pool.tile([P, HALF_HEADS, P], F32, name="do_tile")
                 do_t[(half, q_lo)] = do_tile
+            start = half * ROWS // 2
             copy(
-                out=do_t[(half, q_lo)][:, :, q_hi * ROWS_PER_HEAD : (q_hi + 1) * ROWS_PER_HEAD],
-                in_=dy_banks[(q_lo, q_hi)][:, half * ROWS // 2 : (half + 1) * ROWS // 2].rearrange(
+                out=do_t[(half, q_lo)][:, :count, q_hi * ROWS_PER_HEAD : (q_hi + 1) * ROWS_PER_HEAD],
+                in_=dy_banks[(q_lo, q_hi)][:, start : start + count * ROWS_PER_HEAD].rearrange(
                     "p (g r) -> p g r", r=ROWS_PER_HEAD
                 ),
+            )
+
+        LAST = HEADS - 1
+        do_last = {}
+
+        def empty_bank_last_head(copy, q_lo, q_hi):
+            if q_lo not in do_last:
+                do_last_tile = keep.tile([P, ROWS_PER_HEAD, 2], F32, name="do_last_tile%d" % q_lo)
+                do_last[q_lo] = do_last_tile
+            copy(
+                out=do_last[q_lo][:, :, q_hi],
+                in_=dy_banks[(q_lo, q_hi)][:, LAST * ROWS_PER_HEAD : (LAST + 1) * ROWS_PER_HEAD],
             )
 
         out_view = out.rearrange("b g (r a l) e -> (b g) a r (l e)", a=2, l=2)
@@ -173,9 +186,13 @@ def tile_transposedattentiontransformer_pb_s_kernel(
             if head not in products:
                 product_tile = psum_small.tile([P, 2, D], F32, tag="small")
                 products[head] = product_tile
+            if head == LAST:
+                tokens = do_last[q_lo][:].rearrange("p r a -> p (r a)")
+            else:
+                tokens = do_t[(head // HALF_HEADS, q_lo)][:, head % HALF_HEADS, :]
             nc.tensor.matmul(
                 out=products[head][:, q_lo, :],
-                lhsT=do_t[(head // HALF_HEADS, q_lo)][:, head % HALF_HEADS, :],
+                lhsT=tokens,
                 rhs=attn_f32[:, head, :],
                 start=True,
                 stop=True,
@@ -185,6 +202,11 @@ def tile_transposedattentiontransformer_pb_s_kernel(
             result = results.tile([P, 2 * D], F32)
             copy = nc.vector.tensor_copy if head % 2 == 0 else nc.scalar.copy
             copy(out=result[:], in_=products[head][:].rearrange("p l e -> p (l e)"))
+            if head == LAST:
+                nc.sync.dma_start(
+                    out=out.rearrange("b g (p l) e -> (b g) p (l e)", l=2)[head], in_=result[:]
+                )
+                return
             for q_hi in range(2):
                 part = slice(q_hi * ROWS_PER_HEAD, (q_hi + 1) * ROWS_PER_HEAD)
                 nc.sync.dma_start(out=out_view[head, q_hi], in_=result[part, :])
@@ -215,10 +237,10 @@ def tile_transposedattentiontransformer_pb_s_kernel(
         empty_bank(on_vector, 0, 1, 0)
         empty_bank(on_scalar, 0, 1, 1)
         widen_attn(2, 2)
-        empty_bank(on_vector, 1, 0, 0)
-        empty_bank(on_scalar, 1, 0, 1)
-        empty_bank(on_vector, 1, 1, 0)
-        empty_bank(on_scalar, 1, 1, 1)
+        empty_bank(on_vector, 1, 0, 0, HALF_HEADS - 1)
+        empty_bank(on_scalar, 1, 0, 1, HALF_HEADS - 1)
+        empty_bank(on_vector, 1, 1, 0, HALF_HEADS - 1)
+        empty_bank(on_scalar, 1, 1, 1, HALF_HEADS - 1)
         widen_attn(4, 4)
         for q_lo in range(2):
             for head in range(2):
@@ -226,6 +248,10 @@ def tile_transposedattentiontransformer_pb_s_kernel(
                 if q_lo == 1:
                     finish(head)
         for head in range(2, HEADS):
+            if head == HALF_HEADS:
+                for q_lo in range(2):
+                    empty_bank_last_head(on_vector, q_lo, 0)
+                    empty_bank_last_head(on_scalar, q_lo, 1)
             for q_lo in range(2):
                 product(head, q_lo)
             finish(head)

@@ -168,16 +168,27 @@ def tile_transposedattentiontransformer_pb_s_kernel(
             )
 
         LAST = HEADS - 1
-        do_last = {}
+        TAIL_HEADS = 2
+        FIRST_TAIL = HEADS - TAIL_HEADS
+        do_tail = {}
 
-        def empty_bank_last_head(copy, q_lo, q_hi):
-            if q_lo not in do_last:
-                do_last_tile = keep.tile([P, ROWS_PER_HEAD, 2], F32, name="do_last_tile%d" % q_lo)
-                do_last[q_lo] = do_last_tile
+        def empty_bank_tail_heads(copy, q_lo, q_hi):
+            if q_lo not in do_tail:
+                do_tail_tile = keep.tile(
+                    [P, TAIL_HEADS, ROWS_PER_HEAD, 2], F32, name="do_tail_tile%d" % q_lo
+                )
+                do_tail[q_lo] = do_tail_tile
             copy(
-                out=do_last[q_lo][:, :, q_hi],
-                in_=dy_banks[(q_lo, q_hi)][:, LAST * ROWS_PER_HEAD : (LAST + 1) * ROWS_PER_HEAD],
+                out=do_tail[q_lo][:, :, :, q_hi],
+                in_=dy_banks[(q_lo, q_hi)][:, FIRST_TAIL * ROWS_PER_HEAD :].rearrange(
+                    "p (g r) -> p g r", r=ROWS_PER_HEAD
+                ),
             )
+
+        def tokens_of(head, q_lo):
+            if head >= FIRST_TAIL:
+                return do_tail[q_lo][:, head - FIRST_TAIL, :, :].rearrange("p r a -> p (r a)")
+            return do_t[(head // HALF_HEADS, q_lo)][:, head % HALF_HEADS, :]
 
         out_view = out.rearrange("b g (r a l) e -> (b g) a r (l e)", a=2, l=2)
         products = {}
@@ -186,23 +197,19 @@ def tile_transposedattentiontransformer_pb_s_kernel(
             if head not in products:
                 product_tile = psum_small.tile([P, 2, D], F32, tag="small")
                 products[head] = product_tile
-            if head == LAST:
-                tokens = do_last[q_lo][:].rearrange("p r a -> p (r a)")
-            else:
-                tokens = do_t[(head // HALF_HEADS, q_lo)][:, head % HALF_HEADS, :]
             nc.tensor.matmul(
                 out=products[head][:, q_lo, :],
-                lhsT=tokens,
+                lhsT=tokens_of(head, q_lo),
                 rhs=attn_f32[:, head, :],
                 start=True,
                 stop=True,
             )
 
         def finish(head):
-            result = results.tile([P, 2 * D], F32)
+            result = results.tile([P, 2 * D], F32, tag="result")
             copy = nc.vector.tensor_copy if head % 2 == 0 else nc.scalar.copy
             copy(out=result[:], in_=products[head][:].rearrange("p l e -> p (l e)"))
-            if head == LAST:
+            if head >= FIRST_TAIL:
                 nc.sync.dma_start(
                     out=out.rearrange("b g (p l) e -> (b g) p (l e)", l=2)[head], in_=result[:]
                 )
@@ -210,6 +217,21 @@ def tile_transposedattentiontransformer_pb_s_kernel(
             for q_hi in range(2):
                 part = slice(q_hi * ROWS_PER_HEAD, (q_hi + 1) * ROWS_PER_HEAD)
                 nc.sync.dma_start(out=out_view[head, q_hi], in_=result[part, :])
+
+        last_view = out.rearrange("b g (p l) e -> (b g) l p e", l=2)
+
+        def last_head_part(copy, q_lo):
+            part_product = psum_small.tile([P, D], F32, tag="small")
+            nc.tensor.matmul(
+                out=part_product[:],
+                lhsT=tokens_of(LAST, q_lo),
+                rhs=attn_f32[:, LAST, :],
+                start=True,
+                stop=True,
+            )
+            part_result = results.tile([P, D], F32, tag="result")
+            copy(out=part_result[:], in_=part_product[:])
+            nc.sync.dma_start(out=last_view[LAST, q_lo], in_=part_result[:])
 
         on_vector = nc.vector.tensor_copy
         on_scalar = nc.scalar.copy
@@ -237,21 +259,23 @@ def tile_transposedattentiontransformer_pb_s_kernel(
         empty_bank(on_vector, 0, 1, 0)
         empty_bank(on_scalar, 0, 1, 1)
         widen_attn(2, 2)
-        empty_bank(on_vector, 1, 0, 0, HALF_HEADS - 1)
-        empty_bank(on_scalar, 1, 0, 1, HALF_HEADS - 1)
-        empty_bank(on_vector, 1, 1, 0, HALF_HEADS - 1)
-        empty_bank(on_scalar, 1, 1, 1, HALF_HEADS - 1)
+        empty_bank(on_vector, 1, 0, 0, HALF_HEADS - TAIL_HEADS)
+        empty_bank(on_scalar, 1, 0, 1, HALF_HEADS - TAIL_HEADS)
+        empty_bank(on_vector, 1, 1, 0, HALF_HEADS - TAIL_HEADS)
+        empty_bank(on_scalar, 1, 1, 1, HALF_HEADS - TAIL_HEADS)
         widen_attn(4, 4)
         for q_lo in range(2):
             for head in range(2):
                 product(head, q_lo)
                 if q_lo == 1:
                     finish(head)
-        for head in range(2, HEADS):
-            if head == HALF_HEADS:
+        for head in range(2, LAST):
+            if head == 2:
                 for q_lo in range(2):
-                    empty_bank_last_head(on_vector, q_lo, 0)
-                    empty_bank_last_head(on_scalar, q_lo, 1)
+                    empty_bank_tail_heads(on_vector, q_lo, 0)
+                    empty_bank_tail_heads(on_scalar, q_lo, 1)
             for q_lo in range(2):
                 product(head, q_lo)
             finish(head)
+        last_head_part(on_scalar, 0)
+        last_head_part(on_vector, 1)

@@ -24,6 +24,7 @@ BYTES = 2 * (ROWS * C + C * C + HEADS * D * D) + 4 * HEADS * HEAD_TOKENS * D
 
 HALF_HEADS = HEADS // 2
 GAP_IDLE_PASSES = 2
+FIRST_IDLE_MATMULS = 2
 
 
 def tile_transposedattentiontransformer_pb_s_kernel(
@@ -39,6 +40,8 @@ def tile_transposedattentiontransformer_pb_s_kernel(
         tc.psum_pool(name="psum_small", bufs=4) as psum_small,
         tc.manual_schedule(),
     ):
+        zeros = keep.tile([P, P], F32)
+        nc.vector.memset(zeros[:], 0.0)
         identity = keep.tile([P, P], F32)
         make_identity(nc, identity[:])
 
@@ -76,6 +79,12 @@ def tile_transposedattentiontransformer_pb_s_kernel(
                 in_=g_rows[0][:],
             )
         idle_out = psum_dy.tile([P, ROWS], F32, tag="dy")
+
+        def first_idle_matmuls(count):
+            for i in range(count):
+                nc.tensor.matmul(
+                    out=idle_out[:, :P], lhsT=zeros[:], rhs=zeros[:], start=True, stop=True
+                )
 
         def idle_passes(count):
             for i in range(count):
@@ -235,6 +244,7 @@ def tile_transposedattentiontransformer_pb_s_kernel(
 
         on_vector = nc.vector.tensor_copy
         on_scalar = nc.scalar.copy
+        first_idle_matmuls(FIRST_IDLE_MATMULS)
         for rt in range(ROW_TILES):
             transpose_g(rt)
         idle_passes(GAP_IDLE_PASSES)

@@ -164,13 +164,15 @@ def tile_transposedattentiontransformer_pb_s_kernel(
 
         do_t = {}
 
-        def empty_bank(copy, half, q_lo, q_hi, count=HALF_HEADS):
+        def empty_bank(copy, half, q_lo, q_hi, first=0, count=HALF_HEADS):
             if (half, q_lo) not in do_t:
                 do_tile = do_pool.tile([P, HALF_HEADS, P], F32, name="do_tile")
                 do_t[(half, q_lo)] = do_tile
-            start = half * ROWS // 2
+            start = half * ROWS // 2 + first * ROWS_PER_HEAD
             copy(
-                out=do_t[(half, q_lo)][:, :count, q_hi * ROWS_PER_HEAD : (q_hi + 1) * ROWS_PER_HEAD],
+                out=do_t[(half, q_lo)][
+                    :, first : first + count, q_hi * ROWS_PER_HEAD : (q_hi + 1) * ROWS_PER_HEAD
+                ],
                 in_=dy_banks[(q_lo, q_hi)][:, start : start + count * ROWS_PER_HEAD].rearrange(
                     "p (g r) -> p g r", r=ROWS_PER_HEAD
                 ),
@@ -255,35 +257,44 @@ def tile_transposedattentiontransformer_pb_s_kernel(
         quantise_g(ROW_TILES - 1, 1)
         quantise_w(0, 0)
         mx_pass(0, 0)
-        regroup_w_on_vector(1, 0)
         regroup_w_on_scalar(1, 1)
         quantise_w(0, 1)
         mx_pass(0, 1)
-        quantise_w(1, 0)
-        mx_pass(1, 0)
+        regroup_w_on_vector(1, 0)
         quantise_w(1, 1)
         mx_pass(1, 1)
+        quantise_w(1, 0)
+        mx_pass(1, 0)
         widen_attn(0, 2)
-        empty_bank(on_scalar, 0, 0, 0)
-        empty_bank(on_scalar, 0, 0, 1)
-        empty_bank(on_vector, 0, 1, 0)
-        empty_bank(on_scalar, 0, 1, 1)
+        empty_bank(on_scalar, 0, 0, 0, 0, 2)
+        empty_bank(on_scalar, 0, 0, 1, 0, 2)
+        empty_bank(on_scalar, 0, 1, 1, 0, 2)
+        empty_bank(on_vector, 0, 0, 0, 2, 2)
+        empty_bank(on_vector, 0, 1, 0, 0, 2)
+        empty_bank(on_scalar, 0, 0, 1, 2, 2)
+        empty_bank(on_scalar, 0, 1, 1, 2, 2)
         widen_attn(2, 2)
-        empty_bank(on_vector, 1, 0, 0, HALF_HEADS - TAIL_HEADS)
-        empty_bank(on_scalar, 1, 0, 1, HALF_HEADS - TAIL_HEADS)
-        empty_bank(on_vector, 1, 1, 0, HALF_HEADS - TAIL_HEADS)
-        empty_bank(on_scalar, 1, 1, 1, HALF_HEADS - TAIL_HEADS)
+        empty_bank(on_vector, 0, 1, 0, 2, 2)
+        empty_bank(on_scalar, 1, 0, 1, 0, 2)
+        empty_bank(on_scalar, 1, 1, 1, 0, 2)
+        empty_bank(on_vector, 1, 0, 0, 0, 2)
+        empty_bank_tail_heads(on_scalar, 0, 1)
+
+        def two_heads(first):
+            for q_lo in range(2):
+                for head in range(first, first + 2):
+                    product(head, q_lo)
+                    if q_lo == 1:
+                        finish(head)
+
+        two_heads(0)
+        empty_bank(on_vector, 1, 1, 0, 0, 2)
         widen_attn(4, 4)
-        for q_lo in range(2):
-            for head in range(2):
-                product(head, q_lo)
-                if q_lo == 1:
-                    finish(head)
-        for head in range(2, LAST):
-            if head == 2:
-                for q_lo in range(2):
-                    empty_bank_tail_heads(on_vector, q_lo, 0)
-                    empty_bank_tail_heads(on_scalar, q_lo, 1)
+        empty_bank_tail_heads(on_vector, 0, 0)
+        empty_bank_tail_heads(on_scalar, 1, 1)
+        two_heads(2)
+        empty_bank_tail_heads(on_vector, 1, 0)
+        for head in range(HALF_HEADS, LAST):
             for q_lo in range(2):
                 product(head, q_lo)
             finish(head)

@@ -257,14 +257,14 @@ def tile_transposedattentiontransformer_pb_s_kernel(
         quantise_g(ROW_TILES - 1, 1)
         quantise_w(0, 0)
         mx_pass(0, 0)
+        regroup_w_on_vector(1, 0)
         regroup_w_on_scalar(1, 1)
         quantise_w(0, 1)
         mx_pass(0, 1)
-        regroup_w_on_vector(1, 0)
-        quantise_w(1, 1)
-        mx_pass(1, 1)
         quantise_w(1, 0)
         mx_pass(1, 0)
+        quantise_w(1, 1)
+        mx_pass(1, 1)
         widen_attn(0, 2)
         empty_bank(on_scalar, 0, 0, 0, 0, 2)
         empty_bank(on_scalar, 0, 0, 1, 0, 2)

@@ -131,8 +131,8 @@ def tile_transposedattentiontransformer_pb_s_kernel(
 
         def regroup_w_on_scalar(q_lo, q_hi):
             nc.scalar.copy(
-                out=w_grouped[:, columns(q_lo, q_hi), :],
-                in_=w_raw[:, :, columns(q_lo, q_hi)].rearrange("p t c -> p c t"),
+                out=w_grouped[:, columns(q_lo, q_hi), :].rearrange("p (c i) t -> p c t i", i=4),
+                in_=w_raw[:, :, columns(q_lo, q_hi)].rearrange("p t (c i) -> p c t i", i=4),
             )
 
         def quantise_w(q_lo, q_hi):

import concourse.mybir as mybir
from concourse.masks import make_identity

F32 = mybir.dt.float32
BF16 = mybir.dt.bfloat16
U32 = mybir.dt.uint32
U8 = mybir.dt.uint8
E4M3_X4 = mybir.dt.float8_e4m3fn_x4
E5M2_X4 = mybir.dt.float8_e5m2_x4

P = 128
PACK = 4
C = 512
D = 128
HEADS = 8
ROWS = 512
ROW_TILES = ROWS // P
ROWS_PER_HEAD = ROWS // HEADS
HEAD_TOKENS = 256

FLOPS = 2 * ROWS * C * C + 2 * HEADS * HEAD_TOKENS * D * D
BYTES = 2 * (ROWS * C + C * C + HEADS * D * D) + 4 * HEADS * HEAD_TOKENS * D


HALF_HEADS = HEADS // 2
GAP_IDLE_PASSES = 2
FIRST_IDLE_MATMULS = 2


def tile_transposedattentiontransformer_pb_s_kernel(
    tc, attn, v, w_proj, b_proj, shortcut, grad_out, out
):
    nc = tc.nc
    with (
        tc.tile_pool(name="keep", bufs=1) as keep,
        tc.tile_pool(name="g_in", bufs=ROW_TILES) as g_in,
        tc.tile_pool(name="do_pool", bufs=4) as do_pool,
        tc.tile_pool(name="results", bufs=HEADS) as results,
        tc.psum_pool(name="psum_dy", bufs=4) as psum_dy,
        tc.psum_pool(name="psum_small", bufs=4) as psum_small,
        tc.manual_schedule(),
    ):
        zeros = keep.tile([P, P], F32)
        nc.vector.memset(zeros[:], 0.0)
        identity = keep.tile([P, P], F32)
        make_identity(nc, identity[:])

        def columns(q_lo, q_hi):
            return slice((2 * q_hi + q_lo) * D, (2 * q_hi + q_lo + 1) * D)

        def heads_of(half):
            return slice(half * HALF_HEADS, (half + 1) * HALF_HEADS)

        g_flat = grad_out.flatten_outer_dims()
        g_rows = []
        for rt in range(ROW_TILES):
            g_tile = g_in.tile([P, C], BF16, name="g_tile", align_bytes=64)
            nc.sync.dma_start(out=g_tile[:], in_=g_flat[rt * P : (rt + 1) * P, :])
            g_rows.append(g_tile)
        w_raw = keep.tile([P, PACK, C], BF16)
        nc.sync.dma_start(out=w_raw[:], in_=w_proj.rearrange("(p t) c -> p t c", t=PACK))
        attn_bf = keep.tile([P, HEADS, D], BF16)
        attn_f32 = keep.tile([P, HEADS, D], F32)
        attn_view = attn.rearrange("b g d e -> d (b g) e")
        for half in range(2):
            nc.sync.dma_start(out=attn_bf[:, heads_of(half), :], in_=attn_view[:, heads_of(half), :])

        idle_g_codes = keep.tile([P, ROWS], U32, align_bytes=64)
        idle_g_scales = keep.tile([P, ROWS], U8, align_bytes=64)
        idle_w_codes = keep.tile([P, D], U32, align_bytes=64)
        idle_w_scales = keep.tile([P, D], U8, align_bytes=64)
        nc.vector.quantize_mx(
            out=idle_w_codes[:].bitcast(E4M3_X4), scales=idle_w_scales[:], in_=g_rows[0][:]
        )
        for rt in range(ROW_TILES):
            nc.vector.quantize_mx(
                out=idle_g_codes[:, rt * P : (rt + 1) * P].bitcast(E5M2_X4),
                scales=idle_g_scales[:, rt * P : (rt + 1) * P],
                in_=g_rows[0][:],
            )
        idle_out = psum_dy.tile([P, ROWS], F32, tag="dy")

        def first_idle_matmuls(count):
            for i in range(count):
                nc.tensor.matmul(
                    out=idle_out[:, :P], lhsT=zeros[:], rhs=zeros[:], start=True, stop=True
                )

        def idle_passes(count):
            for i in range(count):
                nc.tensor.matmul_mx(
                    out=idle_out[:],
                    lhsT=idle_w_codes[:].bitcast(E4M3_X4),
                    lhsT_scale=idle_w_scales[:],
                    rhs=idle_g_codes[:].bitcast(E5M2_X4),
                    rhs_scale=idle_g_scales[:],
                    start=True,
                    stop=True,
                )

        g_grouped = keep.tile([P, ROWS * PACK], BF16, align_bytes=64)
        g_grouped_words = g_grouped[:].bitcast(F32).rearrange("p (r u) -> p r u", u=2)
        g_codes = keep.tile([P, ROWS], U32, align_bytes=64)
        g_scales = keep.tile([P, ROWS], U8, align_bytes=64)

        def transpose_g(rt):
            rows = slice(rt * P, (rt + 1) * P)
            g_words = g_rows[rt][:].bitcast(F32).rearrange("r (p u) -> r u p", u=2)
            g_t = psum_small.tile([P, 2, P], F32, tag="small")
            for u in range(2):
                nc.tensor.transpose(g_t[:, u, :], g_words[:, u, :], identity[:])
            nc.scalar.copy(out=g_grouped_words[:, rows, :], in_=g_t[:].rearrange("p u r -> p r u"))

        def quantise_g(first, count):
            rows = slice(first * P, (first + count) * P)
            nc.vector.quantize_mx(
                out=g_codes[:, rows].bitcast(E5M2_X4),
                scales=g_scales[:, rows],
                in_=g_grouped[:, first * P * PACK : (first + count) * P * PACK],
            )

        w_grouped = keep.tile([P, C, PACK], BF16, align_bytes=64)
        w_codes = keep.tile([P, C], U32, align_bytes=64)
        w_scales = keep.tile([P, C], U8, align_bytes=64)

        def regroup_w_on_vector(q_lo, q_hi):
            nc.vector.tensor_copy(
                out=w_grouped[:, columns(q_lo, q_hi), :].rearrange("p (c i) t -> p c t i", i=4),
                in_=w_raw[:, :, columns(q_lo, q_hi)].rearrange("p t (c i) -> p c t i", i=4),
            )

        def regroup_w_on_scalar(q_lo, q_hi):
            nc.scalar.copy(
                out=w_grouped[:, columns(q_lo, q_hi), :].rearrange("p (c i) t -> p c t i", i=4),
                in_=w_raw[:, :, columns(q_lo, q_hi)].rearrange("p t (c i) -> p c t i", i=4),
            )

        def quantise_w(q_lo, q_hi):
            nc.vector.quantize_mx(
                out=w_codes[:, columns(q_lo, q_hi)].bitcast(E4M3_X4),
                scales=w_scales[:, columns(q_lo, q_hi)],
                in_=w_grouped[:, columns(q_lo, q_hi), :].rearrange("p c t -> p (c t)"),
            )

        def widen_attn(first, count):
            nc.vector.tensor_copy(
                out=attn_f32[:, first : first + count, :], in_=attn_bf[:, first : first + count, :]
            )

        dy_banks = {}

        def mx_pass(q_lo, q_hi):
            dy_t = psum_dy.tile([P, ROWS], F32, tag="dy")
            nc.tensor.matmul_mx(
                out=dy_t[:],
                lhsT=w_codes[:, columns(q_lo, q_hi)].bitcast(E4M3_X4),
                lhsT_scale=w_scales[:, columns(q_lo, q_hi)],
                rhs=g_codes[:].bitcast(E5M2_X4),
                rhs_scale=g_scales[:],
                start=True,
                stop=True,
            )
            dy_banks[(q_lo, q_hi)] = dy_t

        do_t = {}

        def empty_bank(copy, half, q_lo, q_hi, first=0, count=HALF_HEADS):
            if (half, q_lo) not in do_t:
                do_tile = do_pool.tile([P, HALF_HEADS, P], F32, name="do_tile")
                do_t[(half, q_lo)] = do_tile
            start = half * ROWS // 2 + first * ROWS_PER_HEAD
            copy(
                out=do_t[(half, q_lo)][
                    :, first : first + count, q_hi * ROWS_PER_HEAD : (q_hi + 1) * ROWS_PER_HEAD
                ],
                in_=dy_banks[(q_lo, q_hi)][:, start : start + count * ROWS_PER_HEAD].rearrange(
                    "p (g r) -> p g r", r=ROWS_PER_HEAD
                ),
            )

        LAST = HEADS - 1
        TAIL_HEADS = 2
        FIRST_TAIL = HEADS - TAIL_HEADS
        do_tail = {}

        def empty_bank_tail_heads(copy, q_lo, q_hi):
            if q_lo not in do_tail:
                do_tail_tile = keep.tile(
                    [P, TAIL_HEADS, ROWS_PER_HEAD, 2], F32, name="do_tail_tile%d" % q_lo
                )
                do_tail[q_lo] = do_tail_tile
            copy(
                out=do_tail[q_lo][:, :, :, q_hi],
                in_=dy_banks[(q_lo, q_hi)][:, FIRST_TAIL * ROWS_PER_HEAD :].rearrange(
                    "p (g r) -> p g r", r=ROWS_PER_HEAD
                ),
            )

        def tokens_of(head, q_lo):
            if head >= FIRST_TAIL:
                return do_tail[q_lo][:, head - FIRST_TAIL, :, :].rearrange("p r a -> p (r a)")
            return do_t[(head // HALF_HEADS, q_lo)][:, head % HALF_HEADS, :]

        out_view = out.rearrange("b g (r a l) e -> (b g) a r (l e)", a=2, l=2)
        products = {}

        def product(head, q_lo):
            if head not in products:
                product_tile = psum_small.tile([P, 2, D], F32, tag="small")
                products[head] = product_tile
            nc.tensor.matmul(
                out=products[head][:, q_lo, :],
                lhsT=tokens_of(head, q_lo),
                rhs=attn_f32[:, head, :],
                start=True,
                stop=True,
            )

        def finish(head):
            result = results.tile([P, 2 * D], F32, tag="result")
            copy = nc.vector.tensor_copy if head % 2 == 0 else nc.scalar.copy
            copy(out=result[:], in_=products[head][:].rearrange("p l e -> p (l e)"))
            if head >= FIRST_TAIL:
                nc.sync.dma_start(
                    out=out.rearrange("b g (p l) e -> (b g) p (l e)", l=2)[head], in_=result[:]
                )
                return
            for q_hi in range(2):
                part = slice(q_hi * ROWS_PER_HEAD, (q_hi + 1) * ROWS_PER_HEAD)
                nc.sync.dma_start(out=out_view[head, q_hi], in_=result[part, :])

        last_view = out.rearrange("b g (p l) e -> (b g) l p e", l=2)

        def last_head_part(copy, q_lo):
            part_product = psum_small.tile([P, D], F32, tag="small")
            nc.tensor.matmul(
                out=part_product[:],
                lhsT=tokens_of(LAST, q_lo),
                rhs=attn_f32[:, LAST, :],
                start=True,
                stop=True,
            )
            part_result = results.tile([P, D], F32, tag="result")
            copy(out=part_result[:], in_=part_product[:])
            nc.sync.dma_start(out=last_view[LAST, q_lo], in_=part_result[:])

        on_vector = nc.vector.tensor_copy
        on_scalar = nc.scalar.copy
        first_idle_matmuls(FIRST_IDLE_MATMULS)
        for rt in range(ROW_TILES):
            transpose_g(rt)
        idle_passes(GAP_IDLE_PASSES)
        for rt in range(ROW_TILES - 1):
            quantise_g(rt, 1)
        regroup_w_on_vector(0, 0)
        regroup_w_on_scalar(0, 1)
        quantise_g(ROW_TILES - 1, 1)
        quantise_w(0, 0)
        mx_pass(0, 0)
        regroup_w_on_vector(1, 0)
        regroup_w_on_scalar(1, 1)
        quantise_w(0, 1)
        mx_pass(0, 1)
        quantise_w(1, 0)
        mx_pass(1, 0)
        quantise_w(1, 1)
        mx_pass(1, 1)
        widen_attn(0, 2)
        empty_bank(on_scalar, 0, 0, 0, 0, 2)
        empty_bank(on_scalar, 0, 0, 1, 0, 2)
        empty_bank(on_scalar, 0, 1, 1, 0, 2)
        empty_bank(on_vector, 0, 0, 0, 2, 2)
        empty_bank(on_vector, 0, 1, 0, 0, 2)
        empty_bank(on_scalar, 0, 0, 1, 2, 2)
        empty_bank(on_scalar, 0, 1, 1, 2, 2)
        widen_attn(2, 2)
        empty_bank(on_vector, 0, 1, 0, 2, 2)
        empty_bank(on_scalar, 1, 0, 1, 0, 2)
        empty_bank(on_scalar, 1, 1, 1, 0, 2)
        empty_bank(on_vector, 1, 0, 0, 0, 2)
        empty_bank_tail_heads(on_scalar, 0, 1)

        def two_heads(first):
            for q_lo in range(2):
                for head in range(first, first + 2):
                    product(head, q_lo)
                    if q_lo == 1:
                        finish(head)

        two_heads(0)
        empty_bank(on_vector, 1, 1, 0, 0, 2)
        widen_attn(4, 4)
        empty_bank_tail_heads(on_vector, 0, 0)
        empty_bank_tail_heads(on_scalar, 1, 1)
        two_heads(2)
        empty_bank_tail_heads(on_vector, 1, 0)
        for head in range(HALF_HEADS, LAST):
            for q_lo in range(2):
                product(head, q_lo)
            finish(head)
        last_head_part(on_scalar, 0)
        last_head_part(on_vector, 1)
